import numpy as np
import ml_dtypes


def mxq(x, axis, fmt="e4m3"):
    dtype, down = {"e4m3": (ml_dtypes.float8_e4m3fn, 7), "e5m2": (ml_dtypes.float8_e5m2, 14)}[fmt]
    v = np.moveaxis(np.asarray(x, np.float32).astype(ml_dtypes.bfloat16).astype(np.float64), axis, -1)
    blocks = v.reshape(v.shape[:-1] + (-1, 32))
    amax = np.abs(blocks).max(-1, keepdims=True)
    byte = np.maximum(np.where(amax > 0, np.frexp(amax)[1] - 1 + 127, 0) - down, 1)
    scale = np.exp2(byte - 127.0)
    codes = (blocks / scale).astype(np.float32).astype(dtype).astype(np.float64)
    return np.moveaxis((codes * scale).reshape(v.shape), -1, axis)


WIDE = False


def mx_kscale(k):
    if not WIDE:
        return np.ones(k)
    levels = np.array([10, -10, 5, -5, 0])
    if k % 512:
        return np.exp2(np.random.permutation(np.resize(levels, k // 32))).repeat(32)
    a = np.empty((k // 512, 16))
    for p in range(k // 512):
        a[p, :8] = np.random.permutation(np.resize(levels, 8))
        for g in range(8):
            far = levels[np.abs(levels - a[p, g]) >= 10]
            a[p, g + 8] = far[np.random.randint(len(far))]
    return np.exp2(a.ravel()).repeat(32)


BF16 = ml_dtypes.bfloat16


def bf(x):
    return np.asarray(x, np.float32).astype(BF16)


def f64(x):
    return np.asarray(x).astype(np.float64)


B, N, C, F = 4, 32, 1024, 1024
KP = 5 * C
EPS_GN = 1e-5


def draw0():
    s = np.concatenate([np.ones(C), mx_kscale(KP - C)])
    t = mx_kscale(C)
    gap = 0.65 * np.sqrt(2.0 * np.log(N))
    mean = 0.65 * np.random.standard_normal((B, N, C))
    lo = mean - gap - 0.35 * np.random.standard_normal((B, N, C))
    hi = mean + gap + 0.35 * np.random.standard_normal((B, N, C))
    std = 0.8 + 0.1 * np.random.standard_normal((B, N, C))
    return {"x": bf(np.random.standard_normal((B, N, C))),
            "agg": bf(np.concatenate([mean, lo, hi, std], axis=-1) * s[C:]),
            "W_post": bf(np.random.standard_normal((KP, C)) / np.sqrt(KP) / s[:, None] * t),
            "b_post": bf(np.random.standard_normal(C) * 0.5 * t),
            "W_lin": bf(np.random.standard_normal((C, C)) / np.sqrt(C) / t[:, None]),
            "b_lin": bf(np.random.standard_normal(C) * 0.5),
            "gn_weight": bf(1.0 + 0.2 * np.random.standard_normal(C)),
            "gn_bias": bf(0.2 * np.random.standard_normal(C)),
            "gn_alpha": bf(0.6 + 0.2 * np.random.standard_normal(C))}


def core(x, agg, W_post, b_post, W_lin, b_lin, gn_weight, gn_bias, gn_alpha):
    res = f64(x)
    cat = np.concatenate([res, f64(agg)], axis=-1)
    out = (mxq(cat, 2, "e4m3") @ mxq(f64(W_post), 0, "e4m3")) + f64(b_post)
    out = (mxq(out, 2, "e4m3") @ mxq(f64(W_lin), 0, "e4m3")) + f64(b_lin)
    flat = out.reshape(B * N, C)
    mu = flat.mean(axis=0, keepdims=True)
    centered = flat - f64(gn_alpha) * mu
    v = (centered * centered).mean(axis=0, keepdims=True)
    normed = f64(gn_weight) * centered / np.sqrt(v + EPS_GN) + f64(gn_bias)
    return np.maximum(normed, 0.0).reshape(B, N, C) + res


def e4m3fn_bytes(y):
    return np.clip(np.asarray(y, np.float64), -448.0, 448.0).astype(np.float32).astype(ml_dtypes.float8_e4m3fn).view(np.uint8)


def e4m3fn_values(b):
    return np.asarray(b, np.uint8).view(ml_dtypes.float8_e4m3fn).astype(np.float64)


def setup_inputs():
    d = draw0()
    x0 = np.asarray(d['W_lin']).astype(np.float64)
    s = (np.max(np.abs(x0), axis=(1,), keepdims=True) / 448.0).astype(np.float32)
    out = {}
    for k, v in d.items():
        if k == 'W_lin':
            out['W_lin_bytes'] = e4m3fn_bytes(x0 / s.astype(np.float64))
            out['W_lin_scale'] = s
        else:
            out[k] = v
    return out


def reference(x, agg, W_post, b_post, W_lin_bytes, W_lin_scale, b_lin, gn_weight, gn_bias, gn_alpha):
    return core(x, agg, W_post, b_post, e4m3fn_values(W_lin_bytes) * W_lin_scale.astype(np.float64), b_lin, gn_weight, gn_bias, gn_alpha)

from contextlib import ExitStack

import concourse.mybir as mybir
from concourse.masks import make_identity

F32 = mybir.dt.float32
BF16 = mybir.dt.bfloat16
U32 = mybir.dt.uint32
U8 = mybir.dt.uint8
FP8 = mybir.dt.float8_e4m3fn
FP8X4 = mybir.dt.float8_e4m3fn_x4
ACT = mybir.ActivationFunctionType
ALU = mybir.AluOpType

P = 128
K1 = 5120
C = 1024
HALF = 512
EPS = 1e-5
FLOPS = 2 * P * K1 * C + 2 * P * C * C

LAG = 2
VC = {12: 224, 13: 384, 14: 384, 15: 304, 17: 272, 9: 368, 10: 352, 11: 320, 16: 304, 18: 224, 19: 144, 5: 192, 6: 416, 7: 448, 8: 160, 2: 240, 4: 288, 3: 224, 1: 336, 0: 352}
VC_DEFAULT = 256
VC_L = (160, 448, 64, 64, 160, 32)
WIDEN = {11: (2, 3), 12: (0, 1, 7), 13: (4,), 14: (5,), 19: (6,)}
V_WIDEN = (3, 4, 5)
CAT = {4: (0,), 7: (1,), 8: (2, 3), 9: (4,)}
TAIL = 'w60 w61 w70 w71 w80 w90 w81 w91'
DMA_ORDER = 'W0a W0b W0c W1a W1b W2 small x W3 agg0 W4 agg1 W5 WL0 W6 WL1 W7 W8 W9 bp'
PEC = {6: 256, 11: 256, 19: 128, 13: 256, 14: 256}
Z_V = ()


def tile_gnnlayer_pb_kernel(
    tc, x, agg, w_post, b_post, w_lin_bytes, w_lin_scale, b_lin, gn_weight, gn_bias, gn_alpha, out
):
    nc = tc.nc
    xf = x.flatten_outer_dims()
    aggf = agg.flatten_outer_dims()
    outf = out.flatten_outer_dims()

    with ExitStack() as ctx:
        keep = ctx.enter_context(tc.tile_pool(name="keep", bufs=1))
        work = ctx.enter_context(tc.tile_pool(name="work", bufs=5))
        psum = ctx.enter_context(tc.psum_pool(name="psum", bufs=1))
        ctx.enter_context(tc.manual_schedule())

        raws = [keep.tile([P, 4, C], BF16, name="raw%d" % c, align_bytes=64) for c in range(10)]
        x_sb = keep.tile([P, C], BF16, name="x_sb", align_bytes=64)
        agg_sb = keep.tile([P, 4 * C], BF16, name="agg_sb", align_bytes=64)
        bpost_sb = keep.tile([P, C], BF16, name="bpost_sb", align_bytes=64)
        wb = keep.tile([P, 2, 4, C], U8, name="wb", align_bytes=64)
        wl = keep.tile([P, 2, 4, C], BF16, name="wl", align_bytes=64)
        wscale = keep.tile([P, 2, 4], F32, name="wscale")
        rows = keep.tile([P, P], BF16, name="rows")
        cols = keep.tile([P, 32], F32, name="cols")
        ident = keep.tile([P, P], F32, name="ident")
        ident_bf = keep.tile([P, P], BF16, name="ident_bf")
        warm = keep.tile([P, 8], F32, name="warm")

        catg = keep.tile([P, 10, 512], BF16, name="catg", align_bytes=64)
        cat_codes = keep.tile([P, 10 * P], U32, name="cat_codes", align_bytes=64)
        cat_scales = keep.tile([P, 10 * P], U8, name="cat_scales", align_bytes=64)
        w_codes = keep.tile([P, 20, HALF], U32, name="w_codes", align_bytes=64)
        w_scales = keep.tile([P, 20, HALF], U8, name="w_scales", align_bytes=64)
        l_codes = keep.tile([P, 2, C], U32, name="l_codes", align_bytes=64)
        l_scales = keep.tile([P, 2, C], U8, name="l_scales", align_bytes=64)
        h_codes = keep.tile([P, 2, P], U32, name="h_codes", align_bytes=64)
        h_scales = keep.tile([P, 2, P], U8, name="h_scales", align_bytes=64)
        hb = keep.tile([P, 2, HALF], BF16, name="hb", align_bytes=64)
        hg = keep.tile([P, 2, HALF], BF16, name="hg", align_bytes=64)
        z = keep.tile([P, 8, P], F32, name="z")
        o_sb = keep.tile([P, C], F32, name="o_sb")
        stats6 = keep.tile([P, 8, 6], F32, name="stats6")
        mv = keep.tile([P, 8, 2], F32, name="mv")
        oma = keep.tile([P, 8], F32, name="oma")
        bo = keep.tile([P, 8], F32, name="bo")
        sm_g, sm_v = [
            {nm: keep.tile([P, 8], F32, name="%s_%s" % (nm, w)) for nm in ("d", "d1", "d2", "ve", "v", "r", "e", "ge", "A", "B0", "B")}
            for w in ("g", "v")
        ]
        gw, gb = cols[:, 8:16], cols[:, 16:24]

        h_ps = [psum.tile([P, HALF], F32, name="h_ps%d" % g, tag="h%d" % g) for g in range(2)]

        def load_w(c, lo, hi):
            rows_c = w_post[512 * c : 512 * (c + 1), :].rearrange("(p j) n -> p j n", j=4)
            nc.sync.dma_start(out=raws[c][:, :, lo:hi], in_=rows_c[:, :, lo:hi])

        nc.vector.memset(rows[:], 0.0)
        nc.vector.memset(warm[:], 1.0)
        make_identity(nc, ident[:])
        make_identity(nc, ident_bf[:])
        nc.scalar.activation(warm[:, 4:5], warm[:, 0:1], ACT.Abs_reciprocal_sqrt)

        wl_rows = w_lin_bytes.rearrange("(g p t) n -> g p t n", g=2, t=4)
        for item in DMA_ORDER.split(" "):
            if item == "small":
                for k, vec in enumerate((b_lin, gn_weight, gn_bias, gn_alpha)):
                    nc.scalar.dma_start(out=rows[8 * k : 8 * k + 8, :], in_=vec.rearrange("(m p) -> m p", p=P))
                nc.scalar.dma_start(out=wscale[:], in_=w_lin_scale.rearrange("(g p t) o -> p g (t o)", g=2, t=4))
            elif item == "W0a":
                load_w(0, 0, 256)
            elif item == "W0b":
                load_w(0, 256, HALF)
            elif item == "W0c":
                load_w(0, HALF, C)
            elif item[-1] in "ab":
                lo = 0 if item[-1] == "a" else HALF
                load_w(int(item[1:-1]), lo, lo + HALF)
            elif item == "x":
                nc.sync.dma_start(out=x_sb[:], in_=xf)
            elif item == "bp":
                nc.sync.dma_start(out=bpost_sb[:], in_=b_post.partition_broadcast(P))
            elif item in ("agg0", "agg1"):
                s = slice(0, 2 * C) if item == "agg0" else slice(2 * C, 4 * C)
                nc.sync.dma_start(out=agg_sb[:, s], in_=aggf[:, s])
            elif item in ("WL0", "WL1"):
                g = 0 if item == "WL0" else 1
                nc.sync.dma_start(out=wb[:, g], in_=wl_rows[g])
            else:
                load_w(int(item[1:]), 0, C)

        def interleave(engine_copy, dst, src, lo, hi):
            engine_copy(
                out=dst[:, 4 * lo : 4 * hi].rearrange("p (c i t) -> p c t i", i=4, t=4),
                in_=src[:, :, lo:hi].rearrange("p t (c i) -> p c t i", i=4),
            )

        groups = {}

        def unit_src(u):
            if u[0] == "w":
                return raws[u[1]][:, :, HALF * u[2] : HALF * (u[2] + 1)]
            return wl[:, u[1], :, u[2] : u[3]]

        order = []

        turned = {}

        def turn(u, pe):
            bank = psum.tile([P, 4 * pe], BF16, name="turn", tag="o", bufs=3)
            turned[u] = bank
            for k in range(pe // P):
                lo = HALF - pe + k * P
                nc.tensor.matmul(
                    bank[:, 512 * k : 512 * (k + 1)],
                    lhsT=ident_bf[:],
                    rhs=unit_src(u)[:, :, lo : lo + P].rearrange("p t c -> p c t"),
                    start=True,
                    stop=True,
                )

        def unit_copy(u):
            grp = work.tile([P, 2048], BF16, name="grp", tag="grp", align_bytes=64)
            groups[u] = grp
            cut = VC.get(len(order), VC_DEFAULT) if u[0] == "w" else VC_L[len(order) - 20]
            order.append(u)
            if u[0] == "l":
                n = u[3] - u[2]
                interleave(nc.vector.tensor_copy, grp, unit_src(u), 0, cut)
                interleave(nc.scalar.copy, grp, unit_src(u), cut, n)
                return
            cut = min(cut, HALF - PEC.get(len(order) - 1, 0))
            interleave(nc.vector.tensor_copy, grp, unit_src(u), 0, cut)
            pe = PEC.get(len(order) - 1, 0)
            if cut < HALF - pe:
                interleave(nc.scalar.copy, grp, unit_src(u), cut, HALF - pe)
            if pe:
                nc.scalar.copy(out=grp[:, 4 * (HALF - pe) :], in_=turned[u][:])

        def unit_quant(u):
            if u[0] == "w":
                codes, scales, n = w_codes[:, 2 * u[1] + u[2], :], w_scales[:, 2 * u[1] + u[2], :], HALF
            else:
                codes, scales, n = l_codes[:, u[1], u[2] : u[3]], l_scales[:, u[1], u[2] : u[3]], u[3] - u[2]
            nc.vector.quantize_mx(out=codes.bitcast(FP8X4), scales=scales, in_=groups[u][:, 0 : 4 * n])

        def unit_mm(u):
            kind, c, g = u
            if kind != "w":
                return
            nc.tensor.matmul_mx(
                out=h_ps[g][:],
                lhsT=cat_codes[:, c * P : (c + 1) * P].bitcast(FP8X4),
                lhsT_scale=cat_scales[:, c * P : (c + 1) * P],
                rhs=w_codes[:, 2 * c + g, :].bitcast(FP8X4),
                rhs_scale=w_scales[:, 2 * c + g, :],
                start=(c == 0),
                stop=(c == 9),
            )

        cat_banks = {}

        def cat_transpose(b):
            bank = psum.tile([P, 2, 2, P], F32, name="trc", tag="tr", bufs=3)
            cat_banks[b] = bank
            for k in range(2):
                c = 2 * b + k
                words = x_sb[:].bitcast(F32) if c < 2 else agg_sb[:].bitcast(F32)
                base = 256 * (c if c < 2 else c - 2)
                for u in range(2):
                    nc.tensor.transpose(bank[:, k, u, :], words[:, base + u : base + 256 : 2], ident[:])

        def cat_evac(b):
            nc.scalar.copy(
                out=catg[:, 2 * b : 2 * b + 2, :].rearrange("p k w -> p (k w)").bitcast(F32).rearrange("p (k r u) -> p k r u", k=2, u=2),
                in_=cat_banks[b][:].rearrange("p k u r -> p k r u"),
            )

        def cat_quant(b):
            sl = slice(2 * b * P, (2 * b + 2) * P)
            nc.vector.quantize_mx(
                out=cat_codes[:, sl].bitcast(FP8X4),
                scales=cat_scales[:, sl],
                in_=catg[:, 2 * b : 2 * b + 2, :].rearrange("p k w -> p (k w)"),
            )

        def vectors():
            bank = psum.tile([P, P], BF16, name="trv", tag="tr", bufs=3)
            nc.tensor.transpose(bank[:], rows[:], ident_bf[:])
            nc.scalar.copy(out=cols[:], in_=bank[:, 0:32])

        def vectors2():
            nc.vector.tensor_scalar(out=oma[:], in0=cols[:, 24:32], scalar1=-1.0, scalar2=1.0, op0=ALU.mult, op1=ALU.add)
            nc.vector.tensor_tensor(out=bo[:], in0=cols[:, 0:8], in1=oma[:], op=ALU.mult)

        def widen(k):
            g, t = divmod(k, 4)
            src = wb[:, g, t, :].bitcast(FP8)
            if k in V_WIDEN:
                nc.vector.tensor_scalar(out=wl[:, g, t, :], in0=src, scalar1=wscale[:, g, t : t + 1], scalar2=None, op0=ALU.mult)
            else:
                nc.scalar.activation(wl[:, g, t, :], src, ACT.Copy, scale=wscale[:, g, t : t + 1])

        def h_bias(g):
            nc.vector.tensor_tensor(
                out=hb[:, g, :], in0=h_ps[g][:], in1=bpost_sb[:, HALF * g : HALF * (g + 1)], op=ALU.add
            )

        h_banks = {}

        def h_transpose(g):
            bank = psum.tile([P, 2, P], F32, name="trh", tag="tr", bufs=3)
            h_banks[g] = bank
            words = hb[:, g, :].bitcast(F32)
            for u in range(2):
                nc.tensor.transpose(bank[:, u, :], words[:, u : 256 : 2], ident[:])

        def h_evac(g):
            nc.scalar.copy(
                out=hg[:, g, :].bitcast(F32).rearrange("p (r u) -> p r u", u=2),
                in_=h_banks[g][:].rearrange("p u r -> p r u"),
            )

        def h_quant(g):
            nc.vector.quantize_mx(out=h_codes[:, g, :].bitcast(FP8X4), scales=h_scales[:, g, :], in_=hg[:, g, :])

        o_ps = []

        def o_tile(m):
            return o_ps[m // 2][:, m % 2, :] if m < 6 else o_ps[m - 3][:, 0, :]

        def mm2(m):
            for g in range(2):
                nc.tensor.matmul_mx(
                    out=o_tile(m),
                    lhsT=l_codes[:, g, m * P : (m + 1) * P].bitcast(FP8X4),
                    lhsT_scale=l_scales[:, g, m * P : (m + 1) * P],
                    rhs=h_codes[:, g, :].bitcast(FP8X4),
                    rhs_scale=h_scales[:, g, :],
                    start=(g == 0),
                    stop=(g == 1),
                )

        def bn(m):
            nc.vector.bn_stats(stats6[:, m, :], o_tile(m))

        def aggr(m):
            nc.vector.bn_aggr(mv[:, m, :], stats6[:, m, :])

        def chain_first(ms):
            s = slice(ms[0], ms[-1] + 1)
            mean, var = mv[:, s, 0], mv[:, s, 1]
            t = {nm: tile[:, s] for nm, tile in sm_g.items()}
            G = nc.gpsimd
            G.tensor_tensor(out=t["d1"], in0=mean, in1=oma[:, s], op=ALU.mult)
            G.tensor_scalar(out=t["ve"], in0=var, scalar1=1.0, scalar2=EPS, op0=ALU.mult, op1=ALU.add)
            G.tensor_tensor(out=t["d"], in0=t["d1"], in1=bo[:, s], op=ALU.add)
            G.tensor_tensor(out=t["d2"], in0=t["d"], in1=t["d"], op=ALU.mult)
            G.tensor_tensor(out=t["v"], in0=t["d2"], in1=t["ve"], op=ALU.add)
            nc.scalar.activation(t["r"], t["v"], ACT.Abs_reciprocal_sqrt)
            G.tensor_tensor(out=t["e"], in0=t["d"], in1=mean, op=ALU.subtract)
            G.tensor_tensor(out=t["ge"], in0=t["e"], in1=gw[:, s], op=ALU.mult)
            G.tensor_tensor(out=t["B0"], in0=t["r"], in1=t["ge"], op=ALU.mult)
            G.tensor_tensor(out=t["A"], in0=t["r"], in1=gw[:, s], op=ALU.mult)
            G.tensor_tensor(out=t["B"], in0=t["B0"], in1=gb[:, s], op=ALU.add)

        def chain_last(ms):
            s = slice(ms[0], ms[-1] + 1)
            mean, var = mv[:, s, 0], mv[:, s, 1]
            one = [slice(m, m + 1) for m in ms]
            V = nc.vector

            def d_step():
                for m, q in zip(ms, one):
                    V.tensor_scalar(out=sm_v["d"][:, q], in0=mv[:, m, 0:1], scalar1=oma[:, q], scalar2=bo[:, q], op0=ALU.mult, op1=ALU.add)
                V.tensor_scalar(out=sm_v["ve"][:, s], in0=var, scalar1=EPS, scalar2=None, op0=ALU.add)

            def v_step():
                for q in one:
                    V.scalar_tensor_tensor(out=sm_v["v"][:, q], in0=sm_v["d"][:, q], scalar=sm_v["d"][:, q], in1=sm_v["ve"][:, q], op0=ALU.mult, op1=ALU.add)
                nc.scalar.activation(sm_v["r"][:, s], sm_v["v"][:, s], ACT.Abs_reciprocal_sqrt)

            def ge_step():
                V.tensor_tensor(out=sm_v["e"][:, s], in0=sm_v["d"][:, s], in1=mean, op=ALU.subtract)
                V.tensor_tensor(out=sm_v["ge"][:, s], in0=sm_v["e"][:, s], in1=gw[:, s], op=ALU.mult)

            def a_step():
                V.tensor_tensor(out=sm_v["A"][:, s], in0=sm_v["r"][:, s], in1=gw[:, s], op=ALU.mult)
                for q in one:
                    V.tensor_scalar(out=sm_v["B"][:, q], in0=sm_v["r"][:, q], scalar1=sm_v["ge"][:, q], scalar2=gb[:, q], op0=ALU.mult, op1=ALU.add)

            return d_step, v_step, ge_step, a_step

        def affine(m, on_vector):
            sm = sm_g if m < 4 else sm_v
            src, sc, bi = o_tile(m), sm["A"][:, m : m + 1], sm["B"][:, m : m + 1]
            if on_vector:
                nc.vector.tensor_scalar(out=z[:, m, :], in0=src, scalar1=sc, scalar2=bi, op0=ALU.mult, op1=ALU.add)
            else:
                nc.scalar.activation(z[:, m, :], src, ACT.Identity, bias=bi, scale=sc)

        out_banks = {}

        def out_transpose(ms):
            bank = psum.tile([P, HALF], F32, name="tro", tag="tr", bufs=3)
            out_banks[ms[0]] = bank
            for k, m in enumerate(ms):
                nc.tensor.transpose(bank[:, k * P : (k + 1) * P], z[:, m, :], ident[:])

        def finish(ms):
            n = P * len(ms)
            sl = slice(P * ms[0], P * ms[0] + n)
            nc.vector.scalar_tensor_tensor(
                out=o_sb[:, sl], in0=out_banks[ms[0]][:, 0:n], scalar=0.0, in1=x_sb[:, sl], op0=ALU.max, op1=ALU.add
            )
            nc.sync.dma_start(out=outf[:, sl], in_=o_sb[:, sl])

        units = [("w", c, g) for c in range(6) for g in range(2)]
        units += [(s[0], int(s[1]), int(s[2])) for s in TAIL.split(" ")]
        extra = {i: [] for i in range(len(units) + 4)}
        extra[3] += [vectors]
        extra[4] += [vectors2]
        for st, ks in WIDEN.items():
            extra[st] += [lambda k=k: widen(k) for k in ks]
        for st, bs in CAT.items():
            extra[st] += [lambda b=b: cat_transpose(b) for b in bs] + [lambda b=b: cat_evac(b) for b in bs]
            extra[st + 1] += [lambda b=b: cat_quant(b) for b in bs]
        first_mm = max(CAT) + 2

        pending = []
        for i, u in enumerate(units):
            unit_copy(u)
            if i + 1 in PEC:
                turn(units[i + 1], PEC[i + 1])
            if i - LAG >= 0:
                unit_quant(units[i - LAG])
                pending.append(units[i - LAG])
            if i >= first_mm:
                for q in pending:
                    unit_mm(q)
                pending = []
            for f in extra[i]:
                f()
        if LAG == 1:
            pass

        A0, A1, B0, B1, C0, C1 = [("l", g, lo, hi) for lo, hi in ((0, 512), (512, 768), (768, 1024)) for g in range(2)]
        unit_copy(A0)
        unit_quant(units[18])
        unit_mm(units[18])
        h_bias(0)
        h_transpose(0)
        unit_quant(units[19])
        unit_mm(units[19])
        h_evac(0)
        unit_copy(A1)
        h_bias(1)
        h_transpose(1)
        unit_quant(A0)
        h_quant(0)
        unit_copy(B0)
        h_evac(1)
        unit_quant(A1)
        unit_copy(B1)
        h_quant(1)
        for k in range(3):
            o_ps.append(psum.tile([P, 2, P], F32, name="o_ps%d" % k, tag="o", bufs=3))
        for k in range(2):
            o_ps.append(psum.tile([P, 1, P], F32, name="o_ps%d" % (3 + k), tag="h%d" % k))
        for m in range(4):
            mm2(m)
        unit_quant(B0)
        unit_copy(C0)
        unit_quant(B1)
        mm2(4)
        mm2(5)
        unit_copy(C1)
        for m in range(4):
            bn(m)
        for m in range(4):
            aggr(m)
        chain_first((0, 1, 2, 3))
        unit_quant(C0)
        unit_quant(C1)
        mm2(6)
        mm2(7)
        bn(4)
        bn(5)
        aggr(4)
        aggr(5)
        bn(6)
        bn(7)
        aggr(6)
        aggr(7)
        d_step, v_step, ge_step, a_step = chain_last((4, 5, 6, 7))
        d_step()
        v_step()
        ge_step()
        for m in range(4):
            affine(m, False)
        out_transpose((0, 1))
        out_transpose((2, 3))
        a_step()
        affine(4, False)
        affine(6, True)
        affine(5, False)
        affine(7, True)
        finish((0, 1))
        finish((2, 3))
        out_transpose((4, 5))
        finish((4, 5))
        out_transpose((6, 7))
        finish((6, 7))
